import numpy as np
import ml_dtypes


def mxq(x, axis, fmt="e4m3"):
    dtype, down = {"e4m3": (ml_dtypes.float8_e4m3fn, 7), "e5m2": (ml_dtypes.float8_e5m2, 14)}[fmt]
    v = np.moveaxis(np.asarray(x, np.float32).astype(ml_dtypes.bfloat16).astype(np.float64), axis, -1)
    blocks = v.reshape(v.shape[:-1] + (-1, 32))
    amax = np.abs(blocks).max(-1, keepdims=True)
    byte = np.maximum(np.where(amax > 0, np.frexp(amax)[1] - 1 + 127, 0) - down, 1)
    scale = np.exp2(byte - 127.0)
    codes = (blocks / scale).astype(np.float32).astype(dtype).astype(np.float64)
    return np.moveaxis((codes * scale).reshape(v.shape), -1, axis)


WIDE = False


def mx_kscale(k):
    if not WIDE:
        return np.ones(k)
    levels = np.array([10, -10, 5, -5, 0])
    if k % 512:
        return np.exp2(np.random.permutation(np.resize(levels, k // 32))).repeat(32)
    a = np.empty((k // 512, 16))
    for p in range(k // 512):
        a[p, :8] = np.random.permutation(np.resize(levels, 8))
        for g in range(8):
            far = levels[np.abs(levels - a[p, g]) >= 10]
            a[p, g + 8] = far[np.random.randint(len(far))]
    return np.exp2(a.ravel()).repeat(32)


BF16 = ml_dtypes.bfloat16


def bf(x):
    return np.asarray(x, np.float32).astype(BF16)


def f64(x):
    return np.asarray(x).astype(np.float64)


E2M1 = np.array([0.0, 0.5, 1.0, 1.5, 2.0, 3.0, 4.0, 6.0, -0.0, -0.5, -1.0, -1.5, -2.0, -3.0, -4.0, -6.0])


def pack_weight(w, fmt):
    k, n = w.shape
    w = f64(bf(w)).reshape(k // 32, 32, n)
    amax = np.abs(w).max(1)
    if fmt == "e4m3":
        byte = np.frexp(amax)[1] - 1 + 127 - 7
    else:
        mant, ex = np.frexp(amax / 6.0)
        byte = np.where(mant > 0.5, ex, ex - 1) + 127
    byte = np.clip(np.where(amax > 0, byte, 1), 1, 254)
    scaled = (w * np.exp2(127.0 - byte)[:, None, :]).reshape(k, n).astype(np.float32)
    by_word = np.ascontiguousarray(scaled.reshape(k // 512, 128, 4, n).transpose(0, 1, 3, 2))
    if fmt == "e4m3":
        words = by_word.astype(ml_dtypes.float8_e4m3fn).view(np.uint8)
    else:
        c = by_word.astype(ml_dtypes.float4_e2m1fn).view(np.uint8) & 0xF
        words = c[..., 0::2] | (c[..., 1::2] << 4)
    return np.ascontiguousarray(words), np.ascontiguousarray(byte.astype(np.uint8).reshape(k // 512, 16, n))


def unpack_weight(words, scales, fmt):
    g, p, n, _ = words.shape
    if fmt == "e4m3":
        vals = np.ascontiguousarray(words).view(ml_dtypes.float8_e4m3fn).astype(np.float64)
    else:
        nib = np.empty((g, p, n, 4), np.uint8)
        nib[..., 0::2] = words & 0xF
        nib[..., 1::2] = words >> 4
        vals = E2M1[nib]
    vals = vals * np.repeat(np.exp2(scales.astype(np.float64) - 127.0), 8, axis=1)[..., None]
    return vals.transpose(0, 1, 3, 2).reshape(g * 512, n)
def pack4(w):
    words, scales = pack_weight(w, "e2m1")
    return words.reshape(words.shape[0], 128, -1), scales


def unpack4(words, scales):
    return unpack_weight(words.reshape(words.shape[0], 128, -1, 2), scales, "e2m1")


B, S, D_MODEL, H, NOPE, ROPE = 1, 512, 2048, 4, 256, 128
DK = D_MODEL // H
LAT = 3 * DK
D_HEAD = NOPE + ROPE
D_LATENT = H * D_HEAD
ROT_DIM = 2 * ((ROPE // 2) // 2)
EPS = 1e-6


def rmsnorm(x, w):
    return x * (1.0 / np.sqrt(np.mean(x * x, axis=-1, keepdims=True) + EPS)) * w


def apply_rope(x):
    inv_freq = 1.0 / (10000.0 ** (np.arange(0, ROT_DIM, 2) / ROT_DIM))
    freqs = np.arange(x.shape[-2])[:, None] * inv_freq[None, :]
    freqs = np.repeat(freqs, 2, axis=-1)
    cos, sin = np.cos(freqs), np.sin(freqs)
    xl, xr = x[..., :ROT_DIM], x[..., ROT_DIM:]
    x1, x2 = xl[..., 0::2], xl[..., 1::2]
    rot = np.stack([-x2, x1], axis=-1).reshape(xl.shape)
    return np.concatenate([xl * cos + rot * sin, xr], axis=-1)


def to_heads(t):
    return t.reshape(B, S, D_HEAD, H).transpose(0, 3, 1, 2)


def draw0():
    s, t = mx_kscale(D_MODEL), mx_kscale(LAT)
    x = bf(np.random.standard_normal((B, S, D_MODEL)) * s)
    w_down_words, w_down_scales = pack4(np.random.standard_normal((D_MODEL, LAT)) / np.sqrt(D_MODEL) / s[:, None])
    rms_w = bf((1.0 + 0.1 * np.random.standard_normal(LAT)) * t)
    w_up_words, w_up_scales = pack4(np.random.standard_normal((LAT, 3 * D_LATENT)) * 1.25 / np.sqrt(LAT) / t[:, None])
    return {"x": x,
            "w_down_words": w_down_words,
            "w_down_scales": w_down_scales,
            "rms_w": rms_w,
            "w_up_words": w_up_words,
            "w_up_scales": w_up_scales}


def core(x, w_down_words, w_down_scales, rms_w, w_up_words, w_up_scales):
    h = mxq(f64(x), 2, "e4m3") @ unpack4(w_down_words, w_down_scales)
    h = rmsnorm(h, f64(rms_w))
    qkv = mxq(h, 2, "e4m3") @ unpack4(w_up_words, w_up_scales)
    q, k, v = np.split(qkv, 3, axis=-1)
    q, k, v = to_heads(q), to_heads(k), to_heads(v)
    q_nope, q_rope = q[..., :NOPE], q[..., NOPE:]
    k_nope, k_rope = k[..., :NOPE], k[..., NOPE:]
    q_rope = apply_rope(q_rope)
    k_rope = apply_rope(k_rope)
    return (np.ascontiguousarray(q_nope), q_rope, np.ascontiguousarray(k_nope), k_rope, np.ascontiguousarray(v))


def e4m3fn_bytes(y):
    return np.clip(np.asarray(y, np.float64), -448.0, 448.0).astype(np.float32).astype(ml_dtypes.float8_e4m3fn).view(np.uint8)


def e4m3fn_values(b):
    return np.asarray(b, np.uint8).view(ml_dtypes.float8_e4m3fn).astype(np.float64)


def setup_inputs():
    d = draw0()
    x0 = np.asarray(d['x']).astype(np.float64)
    s = (np.max(np.abs(x0), axis=(0, 1), keepdims=True) / 448.0).astype(np.float32)
    out = {}
    for k, v in d.items():
        if k == 'x':
            out['x_bytes'] = e4m3fn_bytes(x0 / s.astype(np.float64))
            out['x_scale'] = s
        else:
            out[k] = v
    return out


def reference(x_bytes, x_scale, w_down_words, w_down_scales, rms_w, w_up_words, w_up_scales):
    return core(e4m3fn_values(x_bytes) * x_scale.astype(np.float64), w_down_words, w_down_scales, rms_w, w_up_words, w_up_scales)

@@ -1,0 +1,402 @@
+import math
+from contextlib import ExitStack
+
+import concourse.mybir as mybir
+from concourse.masks import make_identity
+
+F32 = mybir.dt.float32
+BF16 = mybir.dt.bfloat16
+I32 = mybir.dt.int32
+U32 = mybir.dt.uint32
+U8 = mybir.dt.uint8
+FP8 = mybir.dt.float8_e4m3fn
+FP8X4 = mybir.dt.float8_e4m3fn_x4
+FP4X4 = mybir.dt.float4_e2m1fn_x4
+ALU = mybir.AluOpType
+ACT = mybir.ActivationFunctionType
+AX = mybir.AxisListType
+
+P = 128
+S, D_MODEL, LAT, HEADS, D_HEAD = 512, 2048, 1536, 4, 384
+D_OUT = 3 * HEADS * D_HEAD
+NB = S // P
+G1 = D_MODEL // 512
+G2 = LAT // 512
+ROT = 64
+PAIRS = ROT // 2
+EPS = 1e-6
+TWO_PI_HI = 6.28125
+TWO_PI_LO = 2.0 * math.pi - TWO_PI_HI
+
+FLOPS = 2 * S * D_MODEL * LAT + 2 * S * LAT * D_OUT
+
+
+def tile_mhlattention_pa_w4_kernel(
+    tc, x_bytes, x_scale, w_down_words, w_down_scales, rms_w, w_up_words, w_up_scales,
+    q_nope, q_rope, k_nope, k_rope, v_out,
+):
+    nc = tc.nc
+    with ExitStack() as ctx:
+        keep = ctx.enter_context(tc.tile_pool(name="keep", bufs=1))
+        flow = ctx.enter_context(tc.tile_pool(name="flow", bufs=3))
+        work = ctx.enter_context(tc.psum_pool(name="work", bufs=6))
+        turn = ctx.enter_context(tc.psum_pool(name="turn", bufs=2))
+        ctx.enter_context(tc.manual_schedule())
+
+        ident = keep.tile([P, P], F32, name="ident")
+        pos = keep.tile([P, NB], F32, name="pos")
+        nhalf = keep.tile([P, 1], F32, name="nhalf")
+        warm = keep.tile([P, 1], F32, name="warm")
+        vs = keep.tile([P, G1 * 4], F32, name="vs")
+        sx = keep.tile([P, D_MODEL], F32, name="sx")
+        wg = keep.tile([P, LAT], BF16, name="wg")
+        xb = [keep.tile([P, D_MODEL], U8, name="xb%d" % b) for b in range(NB)]
+        wd = [keep.tile([P, 2 * LAT], U8, name="wd%d" % g, align_bytes=64) for g in range(G1)]
+        wds = keep.tile([P, G1 * LAT], U8, name="wds", align_bytes=64)
+        wu = [keep.tile([P, G2, 1024], U8, name="wu%d" % j, align_bytes=64) for j in range(9)]
+        wus = keep.tile([P, G2 * D_OUT], U8, name="wus", align_bytes=64)
+
+        nc.sync.dma_start(out=vs[:].rearrange("p (g m) -> p g m", m=4), in_=x_scale.rearrange("a o (g p m) -> p (a o g) m", p=P, m=4))
+
+        def load_x(b):
+            nc.sync.dma_start(out=xb[b][:], in_=x_bytes[0, b * P:(b + 1) * P, :])
+
+        def load_scales(dst, src, groups, n):
+            for q in range(4):
+                nc.sync.dma_start(
+                    out=dst[32 * q:32 * q + 4, :].bitcast(I32).rearrange("p (g n) -> p g n", g=groups),
+                    in_=src[:, 4 * q:4 * q + 4, :].bitcast(I32).rearrange("g r n -> r g n"),
+                )
+
+        load_x(0)
+        nc.sync.dma_start(out=wd[0][:], in_=w_down_words[0])
+
+        make_identity(nc, ident[:])
+        nc.vector.memset(warm[:], 0.0)
+        nc.scalar.activation(out=warm[:], in_=warm[:], func=ACT.Sin)
+        nc.vector.memset(wds[:].bitcast(I32), 0)
+        nc.vector.memset(wus[:, 0:5760].bitcast(I32), 0)
+        nc.gpsimd.memset(wus[:, 5760:].bitcast(I32), 0)
+        load_scales(wds, w_down_scales, G1, LAT)
+        for g in range(1, G1):
+            nc.sync.dma_start(out=wd[g][:], in_=w_down_words[g])
+        nc.gpsimd.memset(nhalf[:], -0.5)
+        nc.gpsimd.iota(pos[:], pattern=[[P, NB]], base=0, channel_multiplier=1, allow_small_or_imprecise_dtypes=True)
+
+        ang = keep.tile([P, NB, PAIRS], F32, name="ang")
+        nc.gpsimd.tensor_scalar(out=ang[:, :, 0:1], in0=pos[:].unsqueeze(2), scalar1=1.0, scalar2=0.0, op0=ALU.mult, op1=ALU.add)
+        n = 1
+        while n < PAIRS:
+            nc.gpsimd.tensor_scalar(out=ang[:, :, n:2 * n], in0=ang[:, :, 0:n], scalar1=10000.0 ** (-n / PAIRS), scalar2=0.0, op0=ALU.mult, op1=ALU.add)
+            n = 2 * n
+        turns_i = keep.tile([P, NB * PAIRS], I32, name="turns_i")
+        turns = keep.tile([P, NB * PAIRS], F32, name="turns")
+        red = keep.tile([P, NB * PAIRS], F32, name="red")
+        ang_f = ang[:].rearrange("p b i -> p (b i)")
+
+        def rope_reduce(step):
+            if step == 0:
+                nc.vector.tensor_scalar(out=turns_i[:], in0=ang_f, scalar1=1.0 / (2.0 * math.pi), scalar2=None, op0=ALU.mult)
+            elif step == 1:
+                nc.vector.tensor_copy(out=turns[:], in_=turns_i[:])
+            elif step == 2:
+                nc.vector.scalar_tensor_tensor(out=red[:], in0=turns[:], scalar=-TWO_PI_HI, in1=ang_f, op0=ALU.mult, op1=ALU.add)
+            else:
+                nc.vector.scalar_tensor_tensor(out=red[:], in0=turns[:], scalar=-TWO_PI_LO, in1=red[:], op0=ALU.mult, op1=ALU.add)
+
+        load_x(1)
+        nc.sync.dma_start(out=wg[:], in_=rms_w.partition_broadcast(P))
+        load_scales(wus, w_up_scales, G2, D_OUT)
+
+        def load_wu(j):
+            nc.sync.dma_start(out=wu[j][:], in_=w_up_words[:, :, 1024 * j:1024 * (j + 1)].rearrange("g p n -> p g n"))
+
+        load_wu(0)
+        load_wu(1)
+        load_x(2)
+        for j in range(2, 9):
+            load_wu(j)
+        load_x(3)
+
+        s2 = keep.tile([P, NB * PAIRS], F32, name="s2")
+        s4 = keep.tile([P, NB * PAIRS], F32, name="s4")
+        c2 = keep.tile([P, NB * PAIRS], F32, name="c2")
+        cosd = keep.tile([P, NB, PAIRS, 2], F32, name="cosd")
+        sind = keep.tile([P, NB, PAIRS, 2], F32, name="sind")
+
+        def rope_tables():
+            nc.scalar.activation(out=s2[:], in_=red[:], func=ACT.Sin, scale=0.5)
+            nc.scalar.activation(out=s4[:], in_=red[:], func=ACT.Sin, scale=0.25)
+            nc.gpsimd.tensor_tensor(out=s4[:], in0=s4[:], in1=s4[:], op=ALU.mult)
+            nc.gpsimd.tensor_scalar(out=c2[:], in0=s4[:], scalar1=-2.0, scalar2=1.0, op0=ALU.mult, op1=ALU.add)
+            nc.gpsimd.tensor_tensor(out=c2[:], in0=c2[:], in1=s2[:], op=ALU.mult)
+            nc.gpsimd.tensor_tensor(out=s2[:], in0=s2[:], in1=s2[:], op=ALU.mult)
+            s2_v = s2[:].rearrange("p (b i) -> p b i", b=NB)
+            c2_v = c2[:].rearrange("p (b i) -> p b i", b=NB)
+            for e in range(2):
+                nc.gpsimd.tensor_scalar(out=cosd[:, :, :, e], in0=s2_v, scalar1=-2.0, scalar2=1.0, op0=ALU.mult, op1=ALU.add)
+                nc.gpsimd.tensor_scalar(out=sind[:, :, :, e], in0=c2_v, scalar1=2.0 - 4.0 * e, scalar2=0.0, op0=ALU.mult, op1=ALU.add)
+
+        xc = [keep.tile([P, G1 * P], U32, name="xc%d" % b, align_bytes=64) for b in range(NB)]
+        xcs = [keep.tile([P, G1 * P], U8, name="xcs%d" % b, align_bytes=64) for b in range(NB)]
+        nq = [keep.tile([P, G2 * P], U32, name="nq%d" % b, align_bytes=64) for b in range(NB)]
+        nqs = [keep.tile([P, G2 * P], U8, name="nqs%d" % b, align_bytes=64) for b in range(NB)]
+        xs = {}
+        xt = {}
+        xg = {}
+
+        def scale_spread(g):
+            bank = work.tile([P, 4, P], F32, tag="w", name="spread%d" % g)
+            for m in range(4):
+                nc.tensor.transpose(bank[:, m, :], vs[:, 4 * g + m:4 * g + m + 1].to_broadcast([P, P]), ident[:])
+            return bank
+
+        def scale_copy(g, bank):
+            nc.scalar.copy(out=sx[:, 512 * g:512 * (g + 1)].rearrange("q (p m) -> q p m", m=4), in_=bank[:].rearrange("q m p -> q p m"))
+
+        def x_prod(b, g):
+            t = flow.tile([P, 512], BF16, tag="xs", name="xs%d_%d" % (b, g), bufs=5)
+            nc.vector.tensor_tensor(out=t[:], in0=xb[b][:, 512 * g:512 * (g + 1)].bitcast(FP8), in1=sx[:, 512 * g:512 * (g + 1)], op=ALU.mult)
+            xs[b, g] = t
+
+        def x_turn(b, g0, ng):
+            t = turn.tile([P, 2, 2, P], F32, tag="t", name="xt%d_%d" % (b, g0))
+            for g in range(ng):
+                words = xs[b, g0 + g][:].bitcast(F32)
+                for u in range(2):
+                    nc.tensor.transpose(t[:, g, u, :], words[:, u:256:2], ident[:])
+            xt[b, g0] = t
+
+        def x_copy(b, g0, ng, copy):
+            t = flow.tile([P, 2, P, 4], BF16, tag="xg", name="xg%d_%d" % (b, g0), bufs=4, align_bytes=64)
+            dst = t[:, 0:ng].rearrange("p g n t -> p (g n t)").bitcast(F32).rearrange("p (g n u) -> p g n u", g=ng, u=2)
+            copy(out=dst, in_=xt[b, g0][:, 0:ng].rearrange("p g u n -> p g n u"))
+            xg[b, g0] = t
+
+        def x_quant(b, g0, ng):
+            cols = slice(P * g0, P * (g0 + ng))
+            nc.vector.quantize_mx(out=xc[b][:, cols].bitcast(FP8X4), scales=xcs[b][:, cols], in_=xg[b, g0][:, 0:ng].rearrange("p g n t -> p (g n t)"))
+
+        hb = {}
+
+        def h_open(b):
+            for c in range(G2):
+                t = work.tile([P, 512], F32, tag="w", name="h%d_%d" % (b, c))
+                hb[b, c] = t
+
+        def h_mm(b, c, g):
+            cols = slice(P * g, P * (g + 1))
+            nc.tensor.matmul_mx(
+                out=hb[b, c][:],
+                lhsT=xc[b][:, cols].bitcast(FP8X4), lhsT_scale=xcs[b][:, cols],
+                rhs=wd[g][:, 1024 * c:1024 * (c + 1)].bitcast(FP4X4), rhs_scale=wds[:, LAT * g + 512 * c:LAT * g + 512 * (c + 1)],
+                start=(g == 0), stop=(g == G1 - 1),
+            )
+
+        ss = {}
+        rr = {}
+        nt = {}
+        ntt = {}
+        ng_t = {}
+
+        def square(b, c):
+            if c == 0:
+                ss[b] = keep.tile([P, G2], F32, name="ss%d" % b)
+            junk = flow.tile([P, 512], BF16, tag="junk", name="junk%d_%d" % (b, c), bufs=2)
+            nc.scalar.activation(out=junk[:], in_=hb[b, c][:], func=ACT.Square, accum_out=ss[b][:, c:c + 1])
+
+        def rnorm(b):
+            s = keep.tile([P, 1], F32, name="s%d" % b)
+            m = keep.tile([P, 1], F32, name="m%d" % b)
+            r = keep.tile([P, 1], F32, name="r%d" % b)
+            nc.vector.tensor_reduce(out=s[:], in_=ss[b][:], op=ALU.add, axis=AX.X)
+            nc.gpsimd.tensor_scalar(out=m[:], in0=s[:], scalar1=1.0 / LAT, scalar2=EPS, op0=ALU.mult, op1=ALU.add)
+            nc.gpsimd.tensor_tensor(out=r[:], in0=m[:], in1=nhalf[:], op=ALU.pow)
+            rr[b] = r
+
+        def n_make(b, g):
+            t = flow.tile([P, 2, P, 2], BF16, tag="n", name="n%d_%d" % (b, g), bufs=5)
+            hv = hb[b, g][:].rearrange("p (c u e) -> p u c e", u=2, e=2)
+            wv = wg[:, 512 * g:512 * (g + 1)].rearrange("p (c u e) -> p u c e", u=2, e=2)
+            for u in range(2):
+                nc.vector.scalar_tensor_tensor(out=t[:, u], in0=hv[:, u], scalar=rr[b][:], in1=wv[:, u], op0=ALU.mult, op1=ALU.mult)
+            nt[b, g] = t
+
+        def n_turn(b, g0, ng):
+            t = turn.tile([P, 2, 2, P], F32, tag="t", name="nt%d_%d" % (b, g0))
+            for g in range(ng):
+                words = nt[b, g0 + g][:].rearrange("p u c e -> p (u c e)").bitcast(F32)
+                for u in range(2):
+                    nc.tensor.transpose(t[:, g, u, :], words[:, P * u:P * (u + 1)], ident[:])
+            ntt[b, g0] = t
+
+        def n_copy(b, g0, ng, copy):
+            t = flow.tile([P, 2, P, 4], BF16, tag="xg", name="ng%d_%d" % (b, g0), bufs=4, align_bytes=64)
+            dst = t[:, 0:ng].rearrange("p g n t -> p (g n t)").bitcast(F32).rearrange("p (g n u) -> p g n u", g=ng, u=2)
+            copy(out=dst, in_=ntt[b, g0][:, 0:ng].rearrange("p g u n -> p g n u"))
+            ng_t[b, g0] = t
+
+        def n_quant(b, g0, ng):
+            cols = slice(P * g0, P * (g0 + ng))
+            nc.vector.quantize_mx(out=nq[b][:, cols].bitcast(FP8X4), scales=nqs[b][:, cols], in_=ng_t[b, g0][:, 0:ng].rearrange("p g n t -> p (g n t)"))
+
+        ob = {}
+        ot = {}
+
+        def up_mm(b, j):
+            t = work.tile([P, 512], F32, tag="w", name="o%d_%d" % (b, j))
+            for g in range(G2):
+                cols = slice(P * g, P * (g + 1))
+                nc.tensor.matmul_mx(
+                    out=t[:],
+                    lhsT=nq[b][:, cols].bitcast(FP8X4), lhsT_scale=nqs[b][:, cols],
+                    rhs=wu[j][:, g, :].bitcast(FP4X4), rhs_scale=wus[:, D_OUT * g + 512 * j:D_OUT * g + 512 * (j + 1)],
+                    start=(g == 0), stop=(g == G2 - 1),
+                )
+            ob[b, j] = t
+
+        def evacuate(b, j, copy):
+            rows = slice(P * b, P * (b + 1))
+            heads = ob[b, j][:].rearrange("p (d h) -> p h d", h=HEADS)
+            part, c = divmod(j, 3)
+            if part == 2:
+                if c == 0:
+                    ot[b, "v"] = flow.tile([P, HEADS, 384], F32, tag="ov", name="ov%d" % b, bufs=2)
+                t = ot[b, "v"]
+                copy(out=t[:, :, P * c:P * (c + 1)], in_=heads)
+                if b == NB - 1:
+                    nc.sync.dma_start(out=v_out[0, :, rows, P * c:P * (c + 1)].rearrange("h p d -> p h d"), in_=t[:, :, P * c:P * (c + 1)])
+                elif c == 2:
+                    nc.sync.dma_start(out=v_out[0, :, rows, :].rearrange("h p d -> p h d"), in_=t[:])
+            elif c < 2:
+                if c == 0:
+                    ot[b, part] = flow.tile([P, HEADS, 256], F32, tag="on", name="on%d_%d" % (b, part), bufs=3)
+                t = ot[b, part]
+                copy(out=t[:, :, P * c:P * (c + 1)], in_=heads)
+                if c == 1:
+                    dst = q_nope if part == 0 else k_nope
+                    nc.sync.dma_start(out=dst[0, :, rows, :].rearrange("h p d -> p h d"), in_=t[:])
+            else:
+                t = flow.tile([P, HEADS, P], F32, tag="or", name="or%d_%d" % (b, part), bufs=3)
+                turned = flow.tile([P, HEADS, PAIRS, 2], F32, tag="rt", name="rt%d_%d" % (b, part), bufs=2)
+                straight = flow.tile([P, HEADS, ROT], F32, tag="rs", name="rs%d_%d" % (b, part), bufs=2)
+                cos_b = cosd[:, b].rearrange("p i e -> p (i e)").unsqueeze(1).to_broadcast([P, HEADS, ROT])
+                sin_b = sind[:, b].rearrange("p i e -> p (i e)").unsqueeze(1).to_broadcast([P, HEADS, ROT])
+                nc.vector.tensor_tensor(out=straight[:], in0=heads[:, :, 0:ROT], in1=cos_b, op=ALU.mult)
+                nc.vector.tensor_tensor(out=turned[:].rearrange("p h i e -> p h (i e)"), in0=heads[:, :, 0:ROT], in1=sin_b, op=ALU.mult)
+                nc.scalar.copy(out=t[:, :, ROT:P], in_=heads[:, :, ROT:P])
+                nc.vector.tensor_tensor(
+                    out=t[:, :, 0:ROT].rearrange("p h (i e) -> p h i e", e=2),
+                    in0=straight[:].rearrange("p h (i e) -> p h i e", e=2), in1=turned[:, :, :, ::-1], op=ALU.add)
+                dst = q_rope if part == 0 else k_rope
+                nc.sync.dma_start(out=dst[0, :, rows, :].rearrange("h p d -> p h d"), in_=t[:])
+
+        act = nc.scalar.copy
+        vec = nc.vector.tensor_copy
+
+        spread = [scale_spread(g) for g in range(3)]
+        scale_copy(0, spread[0])
+        scale_copy(1, spread[1])
+        x_prod(0, 0)
+        x_turn(0, 0, 1)
+        scale_copy(2, spread[2])
+        x_copy(0, 0, 1, act)
+        last = scale_spread(3)
+        x_prod(0, 1)
+        scale_copy(3, last)
+        x_quant(0, 0, 1)
+        x_turn(0, 1, 1)
+        x_copy(0, 1, 1, act)
+        h_open(0)
+        x_prod(0, 2)
+        x_quant(0, 1, 1)
+        for c in range(G2):
+            h_mm(0, c, 0)
+        x_turn(0, 2, 1)
+        x_copy(0, 2, 1, act)
+        x_prod(0, 3)
+        x_quant(0, 2, 1)
+        for c in range(G2):
+            h_mm(0, c, 1)
+        x_turn(0, 3, 1)
+        x_copy(0, 3, 1, act)
+        x_prod(1, 0)
+        x_quant(0, 3, 1)
+        for c in range(G2):
+            h_mm(0, c, 2)
+        x_prod(1, 1)
+        x_turn(1, 0, 2)
+        x_copy(1, 0, 2, act)
+        x_prod(1, 2)
+        rope_reduce(0)
+        x_quant(1, 0, 2)
+        rope_reduce(1)
+        for c in range(G2):
+            h_mm(0, c, 3)
+            square(0, c)
+        x_prod(1, 3)
+        rope_reduce(2)
+        x_turn(1, 2, 2)
+        x_copy(1, 2, 2, vec)
+        rope_reduce(3)
+        x_quant(1, 2, 2)
+        rnorm(0)
+        rope_tables()
+        h_open(1)
+        for g in range(2):
+            for c in range(G2):
+                h_mm(1, c, g)
+        n_make(0, 0)
+        n_make(0, 1)
+        h_mm(1, 0, 2)
+        h_mm(1, 0, 3)
+        h_mm(1, 1, 2)
+        h_mm(1, 1, 3)
+        n_turn(0, 0, 1)
+        n_copy(0, 0, 1, act)
+        square(1, 0)
+        n_quant(0, 0, 1)
+        n_make(0, 2)
+        h_mm(1, 2, 2)
+        h_mm(1, 2, 3)
+        n_turn(0, 1, 1)
+        n_copy(0, 1, 1, act)
+        square(1, 1)
+        n_quant(0, 1, 1)
+        n_turn(0, 2, 1)
+        n_copy(0, 2, 1, act)
+        square(1, 2)
+        n_quant(0, 2, 1)
+
+        for b in range(NB):
+            nxt = b + 1 < NB
+            far = b + 2 < NB
+            for j in range(9):
+                up_mm(b, j)
+                if nxt and j == 0:
+                    rnorm(b + 1)
+                if nxt and j < 3:
+                    n_make(b + 1, j)
+                evacuate(b, j, vec if b == NB - 1 and j in (1, 4, 7) else act)
+                if nxt and j == 3:
+                    n_turn(b + 1, 0, 2)
+                    n_turn(b + 1, 2, 1)
+                    n_copy(b + 1, 0, 2, act)
+                    n_copy(b + 1, 2, 1, act)
+                    n_quant(b + 1, 0, 2)
+                    n_quant(b + 1, 2, 1)
+                if far and j >= 1 and j < 5:
+                    x_prod(b + 2, j - 1)
+                if far and j == 6:
+                    x_turn(b + 2, 0, 2)
+                    x_turn(b + 2, 2, 2)
+                    x_copy(b + 2, 0, 2, act)
+                    x_copy(b + 2, 2, 2, act)
+                    x_quant(b + 2, 0, 2)
+                    x_quant(b + 2, 2, 2)
+            if far:
+                h_open(b + 2)
+                for c in range(G2):
+                    for g in range(G1):
+                        h_mm(b + 2, c, g)
+                    square(b + 2, c)

@@ -48,10 +48,12 @@ def tile_mhlattention_pa_w4_kernel(
         nhalf = keep.tile([P, 1], F32, name="nhalf")
         warm = keep.tile([P, 1], F32, name="warm")
         vs = keep.tile([P, G1 * 4], F32, name="vs")
+        gain = keep.tile([P, LAT], BF16, name="gain")
+        ones = keep.tile([P, 512], BF16, name="ones")
         sx = keep.tile([P, D_MODEL], F32, name="sx")
-        wg = keep.tile([P, LAT], BF16, name="wg")
+        wg = keep.tile([P, LAT], F32, name="wg")
         xb = [keep.tile([P, D_MODEL], U8, name="xb%d" % b) for b in range(NB)]
-        wd = [keep.tile([P, 2 * LAT], U8, name="wd%d" % g, align_bytes=64) for g in range(G1)]
+        wd = [keep.tile([P, G1, 1024], U8, name="wd%d" % c, align_bytes=64) for c in range(G2)]
         wds = keep.tile([P, G1 * LAT], U8, name="wds", align_bytes=64)
         wu = [keep.tile([P, G2, 1024], U8, name="wu%d" % j, align_bytes=64) for j in range(9)]
         wus = keep.tile([P, G2 * D_OUT], U8, name="wus", align_bytes=64)
@@ -61,25 +63,34 @@ def tile_mhlattention_pa_w4_kernel(
         def load_x(b):
             nc.sync.dma_start(out=xb[b][:], in_=x_bytes[0, b * P:(b + 1) * P, :])
 
-        def load_scales(dst, src, groups, n):
-            for q in range(4):
-                nc.sync.dma_start(
-                    out=dst[32 * q:32 * q + 4, :].bitcast(I32).rearrange("p (g n) -> p g n", g=groups),
-                    in_=src[:, 4 * q:4 * q + 4, :].bitcast(I32).rearrange("g r n -> r g n"),
-                )
+        def load_scales(dst, src, runs, n):
+            for g0, g1 in runs:
+                for q in range(4):
+                    nc.sync.dma_start(
+                        out=dst[32 * q:32 * q + 4, n * g0:n * g1].bitcast(I32).rearrange("p (g n) -> p g n", g=g1 - g0),
+                        in_=src[g0:g1, 4 * q:4 * q + 4, :].bitcast(I32).rearrange("g r n -> r g n"),
+                    )
+
+        def load_wd(c):
+            nc.sync.dma_start(out=wd[c][:], in_=w_down_words[:, :, 1024 * c:1024 * (c + 1)].rearrange("g p n -> p g n"))
 
         load_x(0)
-        nc.sync.dma_start(out=wd[0][:], in_=w_down_words[0])
+        load_wd(0)
 
-        make_identity(nc, ident[:])
         nc.vector.memset(warm[:], 0.0)
         nc.scalar.activation(out=warm[:], in_=warm[:], func=ACT.Sin)
-        nc.vector.memset(wds[:].bitcast(I32), 0)
+        nc.vector.memset(wds[:, 0:3072].bitcast(I32), 0)
+        nc.gpsimd.memset(wds[:, 3072:].bitcast(I32), 0)
+        make_identity(nc, ident[:])
+        nc.vector.memset(ones[:], 1.0)
+        nc.gpsimd.memset(gain[:], 0.0)
         nc.vector.memset(wus[:, 0:5760].bitcast(I32), 0)
         nc.gpsimd.memset(wus[:, 5760:].bitcast(I32), 0)
-        load_scales(wds, w_down_scales, G1, LAT)
-        for g in range(1, G1):
-            nc.sync.dma_start(out=wd[g][:], in_=w_down_words[g])
+        load_scales(wds, w_down_scales, [(0, G1)], LAT)
+        load_wd(1)
+        load_wd(2)
+        load_x(1)
+        nc.sync.dma_start(out=gain[0:1, :], in_=rms_w.unsqueeze(0))
         nc.gpsimd.memset(nhalf[:], -0.5)
         nc.gpsimd.iota(pos[:], pattern=[[P, NB]], base=0, channel_multiplier=1, allow_small_or_imprecise_dtypes=True)
 
@@ -104,9 +115,7 @@ def tile_mhlattention_pa_w4_kernel(
             else:
                 nc.vector.scalar_tensor_tensor(out=red[:], in0=turns[:], scalar=-TWO_PI_LO, in1=red[:], op0=ALU.mult, op1=ALU.add)
 
-        load_x(1)
-        nc.sync.dma_start(out=wg[:], in_=rms_w.partition_broadcast(P))
-        load_scales(wus, w_up_scales, G2, D_OUT)
+        load_scales(wus, w_up_scales, [(0, 1), (1, 2), (2, 3)], D_OUT)
 
         def load_wu(j):
             nc.sync.dma_start(out=wu[j][:], in_=w_up_words[:, :, 1024 * j:1024 * (j + 1)].rearrange("g p n -> p g n"))
@@ -154,6 +163,16 @@ def tile_mhlattention_pa_w4_kernel(
         def scale_copy(g, bank):
             nc.scalar.copy(out=sx[:, 512 * g:512 * (g + 1)].rearrange("q (p m) -> q p m", m=4), in_=bank[:].rearrange("q m p -> q p m"))
 
+        def gain_spread(g):
+            bank = work.tile([P, 512], F32, tag="w", name="gain%d" % g)
+            nc.tensor.matmul(bank[:], lhsT=ones[:, 0:P], rhs=gain[:, 512 * g:512 * (g + 1)], start=True, stop=True)
+            nc.scalar.copy(out=wg[:, 512 * g:512 * (g + 1)], in_=bank[:])
+
+        def warm_up(n):
+            bank = work.tile([P, 512], F32, tag="w", name="warmer")
+            for i in range(n):
+                nc.tensor.matmul(bank[:], lhsT=ones[:, 0:P], rhs=ones[:], start=True, stop=True)
+
         def x_prod(b, g):
             t = flow.tile([P, 512], BF16, tag="xs", name="xs%d_%d" % (b, g), bufs=5)
             nc.vector.tensor_tensor(out=t[:], in0=xb[b][:, 512 * g:512 * (g + 1)].bitcast(FP8), in1=sx[:, 512 * g:512 * (g + 1)], op=ALU.mult)
@@ -189,7 +208,7 @@ def tile_mhlattention_pa_w4_kernel(
             nc.tensor.matmul_mx(
                 out=hb[b, c][:],
                 lhsT=xc[b][:, cols].bitcast(FP8X4), lhsT_scale=xcs[b][:, cols],
-                rhs=wd[g][:, 1024 * c:1024 * (c + 1)].bitcast(FP4X4), rhs_scale=wds[:, LAT * g + 512 * c:LAT * g + 512 * (c + 1)],
+                rhs=wd[c][:, g, :].bitcast(FP4X4), rhs_scale=wds[:, LAT * g + 512 * c:LAT * g + 512 * (c + 1)],
                 start=(g == 0), stop=(g == G1 - 1),
             )
 
@@ -294,109 +313,136 @@ def tile_mhlattention_pa_w4_kernel(
         act = nc.scalar.copy
         vec = nc.vector.tensor_copy
 
+        warm_up(3)
         spread = [scale_spread(g) for g in range(3)]
-        scale_copy(0, spread[0])
-        scale_copy(1, spread[1])
+        for g in range(3):
+            scale_copy(g, spread[g])
         x_prod(0, 0)
         x_turn(0, 0, 1)
-        scale_copy(2, spread[2])
         x_copy(0, 0, 1, act)
         last = scale_spread(3)
-        x_prod(0, 1)
         scale_copy(3, last)
+        x_prod(0, 1)
         x_quant(0, 0, 1)
         x_turn(0, 1, 1)
         x_copy(0, 1, 1, act)
-        h_open(0)
         x_prod(0, 2)
         x_quant(0, 1, 1)
-        for c in range(G2):
-            h_mm(0, c, 0)
         x_turn(0, 2, 1)
         x_copy(0, 2, 1, act)
         x_prod(0, 3)
         x_quant(0, 2, 1)
-        for c in range(G2):
-            h_mm(0, c, 1)
         x_turn(0, 3, 1)
         x_copy(0, 3, 1, act)
-        x_prod(1, 0)
         x_quant(0, 3, 1)
-        for c in range(G2):
-            h_mm(0, c, 2)
-        x_prod(1, 1)
-        x_turn(1, 0, 2)
-        x_copy(1, 0, 2, act)
-        x_prod(1, 2)
-        rope_reduce(0)
-        x_quant(1, 0, 2)
-        rope_reduce(1)
-        for c in range(G2):
-            h_mm(0, c, 3)
+        x_prod(1, 0)
+        for g in range(G2):
+            gain_spread(g)
+        h_open(0)
+        for c in range(2):
+            for g in range(G1):
+                h_mm(0, c, g)
             square(0, c)
+        x_prod(1, 1)
+        rope_reduce(0)
+        x_turn(1, 0, 2)
+        x_prod(1, 2)
+        rope_reduce(1)
+        x_copy(1, 0, 2, vec)
+        for g in range(G1):
+            h_mm(0, 2, g)
         x_prod(1, 3)
-        rope_reduce(2)
+        x_quant(1, 0, 2)
         x_turn(1, 2, 2)
+        rope_reduce(2)
         x_copy(1, 2, 2, vec)
-        rope_reduce(3)
+        square(0, 2)
         x_quant(1, 2, 2)
         rnorm(0)
+        rope_reduce(3)
         rope_tables()
-        h_open(1)
-        for g in range(2):
-            for c in range(G2):
-                h_mm(1, c, g)
         n_make(0, 0)
         n_make(0, 1)
-        h_mm(1, 0, 2)
-        h_mm(1, 0, 3)
-        h_mm(1, 1, 2)
-        h_mm(1, 1, 3)
-        n_turn(0, 0, 1)
-        n_copy(0, 0, 1, act)
-        square(1, 0)
-        n_quant(0, 0, 1)
         n_make(0, 2)
-        h_mm(1, 2, 2)
-        h_mm(1, 2, 3)
-        n_turn(0, 1, 1)
-        n_copy(0, 1, 1, act)
-        square(1, 1)
-        n_quant(0, 1, 1)
+        h_open(1)
+        for c in range(2):
+            for g in range(G1):
+                h_mm(1, c, g)
+        n_turn(0, 0, 2)
         n_turn(0, 2, 1)
-        n_copy(0, 2, 1, act)
-        square(1, 2)
+        n_copy(0, 0, 2, act)
+        n_copy(0, 2, 1, vec)
+        square(1, 0)
+        n_quant(0, 0, 2)
         n_quant(0, 2, 1)
+        for g in range(G1):
+            h_mm(1, 2, g)
+        square(1, 1)
+        square(1, 2)
+
+        def norm_turn(b):
+            n_turn(b, 0, 2)
+            n_turn(b, 2, 1)
+            n_copy(b, 0, 2, act)
+            n_copy(b, 2, 1, act)
+
+        def norm_quant(b):
+            n_quant(b, 0, 2)
+            n_quant(b, 2, 1)
+
+        def x_turns(b):
+            x_turn(b, 0, 2)
+            x_turn(b, 2, 2)
+            x_copy(b, 0, 2, act)
+            x_copy(b, 2, 2, act)
+
+        def x_quants(b):
+            x_quant(b, 0, 2)
+            x_quant(b, 2, 2)
+
+        def down(b):
+            h_open(b)
+            for c in range(G2):
+                for g in range(G1):
+                    h_mm(b, c, g)
+                square(b, c)
+
+        before = {}
+        after = {}
+
+        def at(table, b, j, fn, *args):
+            table.setdefault((b, j), []).append((fn, args))
+
+        at(after, 0, 0, rnorm, 1)
+        at(after, 0, 0, n_make, 1, 0)
+        at(after, 0, 1, n_make, 1, 1)
+        at(before, 0, 2, n_make, 1, 2)
+        at(before, 0, 0, x_prod, 2, 0)
+        at(before, 0, 0, x_prod, 2, 1)
+        at(after, 0, 2, x_prod, 2, 2)
+        at(after, 0, 3, x_prod, 2, 3)
+        at(after, 0, 4, norm_turn, 1)
+        at(before, 0, 5, norm_quant, 1)
+        at(after, 0, 7, x_turns, 2)
+        at(after, 0, 8, x_quants, 2)
+        for b in (1, 2):
+            at(after, b, 1, down, b + 1)
+            at(before, b, 2, rnorm, b + 1)
+            at(before, b, 2, n_make, b + 1, 0)
+            at(after, b, 2, n_make, b + 1, 1)
+            at(after, b, 3, n_make, b + 1, 2)
+            at(after, b, 6, norm_turn, b + 1)
+            at(after, b, 7, norm_quant, b + 1)
+        for g, j in enumerate((0, 0, 1, 1)):
+            at(after, 1, j, x_prod, 3, g)
+        at(after, 1, 4, x_turns, 3)
+        at(after, 1, 5, x_quants, 3)
 
         for b in range(NB):
-            nxt = b + 1 < NB
-            far = b + 2 < NB
             for j in range(9):
                 up_mm(b, j)
-                if nxt and j == 0:
-                    rnorm(b + 1)
-                if nxt and j < 3:
-                    n_make(b + 1, j)
+                for fn, args in before.get((b, j), []):
+                    fn(*args)
                 evacuate(b, j, vec if b == NB - 1 and j in (1, 4, 7) else act)
-                if nxt and j == 3:
-                    n_turn(b + 1, 0, 2)
-                    n_turn(b + 1, 2, 1)
-                    n_copy(b + 1, 0, 2, act)
-                    n_copy(b + 1, 2, 1, act)
-                    n_quant(b + 1, 0, 2)
-                    n_quant(b + 1, 2, 1)
-                if far and j >= 1 and j < 5:
-                    x_prod(b + 2, j - 1)
-                if far and j == 6:
-                    x_turn(b + 2, 0, 2)
-                    x_turn(b + 2, 2, 2)
-                    x_copy(b + 2, 0, 2, act)
-                    x_copy(b + 2, 2, 2, act)
-                    x_quant(b + 2, 0, 2)
-                    x_quant(b + 2, 2, 2)
-            if far:
-                h_open(b + 2)
-                for c in range(G2):
-                    for g in range(G1):
-                        h_mm(b + 2, c, g)
-                    square(b + 2, c)
+                for fn, args in after.get((b, j), []):
+                    fn(*args)

@@ -45,11 +45,10 @@ def tile_mhlattention_pa_w4_kernel(
 
         ident = keep.tile([P, P], F32, name="ident")
         pos = keep.tile([P, NB], F32, name="pos")
-        nhalf = keep.tile([P, 1], F32, name="nhalf")
         warm = keep.tile([P, 1], F32, name="warm")
         vs = keep.tile([P, G1 * 4], F32, name="vs")
         gain = keep.tile([P, LAT], BF16, name="gain")
-        ones = keep.tile([P, 512], BF16, name="ones")
+        ones = keep.tile([P, P], BF16, name="ones")
         sx = keep.tile([P, D_MODEL], F32, name="sx")
         wg = keep.tile([P, LAT], F32, name="wg")
         xb = [keep.tile([P, D_MODEL], U8, name="xb%d" % b) for b in range(NB)]
@@ -75,23 +74,20 @@ def tile_mhlattention_pa_w4_kernel(
             nc.sync.dma_start(out=wd[c][:], in_=w_down_words[:, :, 1024 * c:1024 * (c + 1)].rearrange("g p n -> p g n"))
 
         load_x(0)
-        load_wd(0)
-
         nc.vector.memset(warm[:], 0.0)
         nc.scalar.activation(out=warm[:], in_=warm[:], func=ACT.Sin)
-        nc.vector.memset(wds[:, 0:3072].bitcast(I32), 0)
-        nc.gpsimd.memset(wds[:, 3072:].bitcast(I32), 0)
-        make_identity(nc, ident[:])
+        nc.vector.memset(gain[:], 0.0)
         nc.vector.memset(ones[:], 1.0)
-        nc.gpsimd.memset(gain[:], 0.0)
-        nc.vector.memset(wus[:, 0:5760].bitcast(I32), 0)
-        nc.gpsimd.memset(wus[:, 5760:].bitcast(I32), 0)
+        nc.sync.dma_start(out=gain[0:1, :], in_=rms_w.unsqueeze(0))
+        load_wd(0)
+        nc.vector.memset(wds[:].bitcast(I32), 0)
+        nc.gpsimd.memset(wus[:, 9216:].bitcast(I32), 0)
+        nc.vector.memset(wus[:, 0:9216].bitcast(I32), 0)
+        make_identity(nc, ident[:])
         load_scales(wds, w_down_scales, [(0, G1)], LAT)
         load_wd(1)
         load_wd(2)
         load_x(1)
-        nc.sync.dma_start(out=gain[0:1, :], in_=rms_w.unsqueeze(0))
-        nc.gpsimd.memset(nhalf[:], -0.5)
         nc.gpsimd.iota(pos[:], pattern=[[P, NB]], base=0, channel_multiplier=1, allow_small_or_imprecise_dtypes=True)
 
         ang = keep.tile([P, NB, PAIRS], F32, name="ang")
@@ -133,18 +129,23 @@ def tile_mhlattention_pa_w4_kernel(
         cosd = keep.tile([P, NB, PAIRS, 2], F32, name="cosd")
         sind = keep.tile([P, NB, PAIRS, 2], F32, name="sind")
 
-        def rope_tables():
+        def rope_sines():
             nc.scalar.activation(out=s2[:], in_=red[:], func=ACT.Sin, scale=0.5)
             nc.scalar.activation(out=s4[:], in_=red[:], func=ACT.Sin, scale=0.25)
-            nc.gpsimd.tensor_tensor(out=s4[:], in0=s4[:], in1=s4[:], op=ALU.mult)
-            nc.gpsimd.tensor_scalar(out=c2[:], in0=s4[:], scalar1=-2.0, scalar2=1.0, op0=ALU.mult, op1=ALU.add)
-            nc.gpsimd.tensor_tensor(out=c2[:], in0=c2[:], in1=s2[:], op=ALU.mult)
-            nc.gpsimd.tensor_tensor(out=s2[:], in0=s2[:], in1=s2[:], op=ALU.mult)
+            nc.scalar.activation(out=warm[:], in_=warm[:], func=ACT.Sqrt)
+
+        def rope_products():
+            nc.vector.tensor_tensor(out=s4[:], in0=s4[:], in1=s4[:], op=ALU.mult)
+            nc.vector.tensor_scalar(out=c2[:], in0=s4[:], scalar1=-2.0, scalar2=1.0, op0=ALU.mult, op1=ALU.add)
+            nc.vector.tensor_tensor(out=c2[:], in0=c2[:], in1=s2[:], op=ALU.mult)
+            nc.vector.tensor_tensor(out=s2[:], in0=s2[:], in1=s2[:], op=ALU.mult)
+
+        def rope_tables():
             s2_v = s2[:].rearrange("p (b i) -> p b i", b=NB)
             c2_v = c2[:].rearrange("p (b i) -> p b i", b=NB)
             for e in range(2):
-                nc.gpsimd.tensor_scalar(out=cosd[:, :, :, e], in0=s2_v, scalar1=-2.0, scalar2=1.0, op0=ALU.mult, op1=ALU.add)
-                nc.gpsimd.tensor_scalar(out=sind[:, :, :, e], in0=c2_v, scalar1=2.0 - 4.0 * e, scalar2=0.0, op0=ALU.mult, op1=ALU.add)
+                nc.vector.tensor_scalar(out=cosd[:, :, :, e], in0=s2_v, scalar1=-2.0, scalar2=1.0, op0=ALU.mult, op1=ALU.add)
+                nc.vector.tensor_scalar(out=sind[:, :, :, e], in0=c2_v, scalar1=2.0 - 4.0 * e, scalar2=None, op0=ALU.mult)
 
         xc = [keep.tile([P, G1 * P], U32, name="xc%d" % b, align_bytes=64) for b in range(NB)]
         xcs = [keep.tile([P, G1 * P], U8, name="xcs%d" % b, align_bytes=64) for b in range(NB)]
@@ -165,13 +166,16 @@ def tile_mhlattention_pa_w4_kernel(
 
         def gain_spread(g):
             bank = work.tile([P, 512], F32, tag="w", name="gain%d" % g)
-            nc.tensor.matmul(bank[:], lhsT=ones[:, 0:P], rhs=gain[:, 512 * g:512 * (g + 1)], start=True, stop=True)
+            nc.tensor.matmul(bank[:], lhsT=ones[:], rhs=gain[:, 512 * g:512 * (g + 1)], start=True, stop=True)
+            return bank
+
+        def gain_copy(g, bank):
             nc.scalar.copy(out=wg[:, 512 * g:512 * (g + 1)], in_=bank[:])
 
         def warm_up(n):
             bank = work.tile([P, 512], F32, tag="w", name="warmer")
             for i in range(n):
-                nc.tensor.matmul(bank[:], lhsT=ones[:, 0:P], rhs=ones[:], start=True, stop=True)
+                nc.tensor.matmul(bank[:], lhsT=ones[:], rhs=gain[:, 0:512], start=True, stop=True)
 
         def x_prod(b, g):
             t = flow.tile([P, 512], BF16, tag="xs", name="xs%d_%d" % (b, g), bufs=5)
@@ -214,6 +218,7 @@ def tile_mhlattention_pa_w4_kernel(
 
         ss = {}
         rr = {}
+        mm = {}
         nt = {}
         ntt = {}
         ng_t = {}
@@ -224,13 +229,18 @@ def tile_mhlattention_pa_w4_kernel(
             junk = flow.tile([P, 512], BF16, tag="junk", name="junk%d_%d" % (b, c), bufs=2)
             nc.scalar.activation(out=junk[:], in_=hb[b, c][:], func=ACT.Square, accum_out=ss[b][:, c:c + 1])
 
-        def rnorm(b):
+        def rbias(b):
             s = keep.tile([P, 1], F32, name="s%d" % b)
             m = keep.tile([P, 1], F32, name="m%d" % b)
+            nc.vector.tensor_tensor(out=s[:], in0=ss[b][:, 0:1], in1=ss[b][:, 1:2], op=ALU.add)
+            nc.vector.tensor_scalar(out=m[:], in0=s[:], scalar1=1.0 / LAT, scalar2=EPS, op0=ALU.mult, op1=ALU.add)
+            mm[b] = m
+
+        def rnorm(b):
+            t = keep.tile([P, 1], F32, name="t%d" % b)
             r = keep.tile([P, 1], F32, name="r%d" % b)
-            nc.vector.tensor_reduce(out=s[:], in_=ss[b][:], op=ALU.add, axis=AX.X)
-            nc.gpsimd.tensor_scalar(out=m[:], in0=s[:], scalar1=1.0 / LAT, scalar2=EPS, op0=ALU.mult, op1=ALU.add)
-            nc.gpsimd.tensor_tensor(out=r[:], in0=m[:], in1=nhalf[:], op=ALU.pow)
+            nc.scalar.activation(out=t[:], in_=ss[b][:, 2:3], func=ACT.Sqrt, scale=1.0 / LAT, bias=mm[b][:])
+            nc.vector.reciprocal(out=r[:], in_=t[:])
             rr[b] = r
 
         def n_make(b, g):
@@ -313,7 +323,6 @@ def tile_mhlattention_pa_w4_kernel(
         act = nc.scalar.copy
         vec = nc.vector.tensor_copy
 
-        warm_up(3)
         spread = [scale_spread(g) for g in range(3)]
         for g in range(3):
             scale_copy(g, spread[g])
@@ -323,44 +332,49 @@ def tile_mhlattention_pa_w4_kernel(
         last = scale_spread(3)
         scale_copy(3, last)
         x_prod(0, 1)
+        rope_reduce(0)
         x_quant(0, 0, 1)
         x_turn(0, 1, 1)
         x_copy(0, 1, 1, act)
+        warm_up(1)
         x_prod(0, 2)
+        rope_reduce(1)
         x_quant(0, 1, 1)
         x_turn(0, 2, 1)
         x_copy(0, 2, 1, act)
+        warm_up(1)
         x_prod(0, 3)
+        rope_reduce(2)
         x_quant(0, 2, 1)
         x_turn(0, 3, 1)
+        rope_reduce(3)
         x_copy(0, 3, 1, act)
         x_quant(0, 3, 1)
         x_prod(1, 0)
-        for g in range(G2):
-            gain_spread(g)
+        rope_sines()
+        gains = [gain_spread(g) for g in range(G2)]
         h_open(0)
         for c in range(2):
             for g in range(G1):
                 h_mm(0, c, g)
             square(0, c)
         x_prod(1, 1)
-        rope_reduce(0)
         x_turn(1, 0, 2)
         x_prod(1, 2)
-        rope_reduce(1)
         x_copy(1, 0, 2, vec)
+        gain_copy(0, gains[0])
         for g in range(G1):
             h_mm(0, 2, g)
         x_prod(1, 3)
         x_quant(1, 0, 2)
+        rbias(0)
         x_turn(1, 2, 2)
-        rope_reduce(2)
         x_copy(1, 2, 2, vec)
         square(0, 2)
         x_quant(1, 2, 2)
         rnorm(0)
-        rope_reduce(3)
-        rope_tables()
+        gain_copy(1, gains[1])
+        gain_copy(2, gains[2])
         n_make(0, 0)
         n_make(0, 1)
         n_make(0, 2)
@@ -379,6 +393,7 @@ def tile_mhlattention_pa_w4_kernel(
             h_mm(1, 2, g)
         square(1, 1)
         square(1, 2)
+        rope_products()
 
         def norm_turn(b):
             n_turn(b, 0, 2)
@@ -413,20 +428,23 @@ def tile_mhlattention_pa_w4_kernel(
         def at(table, b, j, fn, *args):
             table.setdefault((b, j), []).append((fn, args))
 
-        at(after, 0, 0, rnorm, 1)
-        at(after, 0, 0, n_make, 1, 0)
-        at(after, 0, 1, n_make, 1, 1)
-        at(before, 0, 2, n_make, 1, 2)
         at(before, 0, 0, x_prod, 2, 0)
-        at(before, 0, 0, x_prod, 2, 1)
-        at(after, 0, 2, x_prod, 2, 2)
-        at(after, 0, 3, x_prod, 2, 3)
+        at(before, 0, 0, rbias, 1)
+        at(before, 0, 0, rnorm, 1)
+        at(after, 0, 0, n_make, 1, 0)
+        at(after, 0, 0, n_make, 1, 1)
+        at(after, 0, 1, n_make, 1, 2)
+        at(after, 0, 1, rope_tables)
+        at(after, 0, 2, x_prod, 2, 1)
+        at(after, 0, 3, x_prod, 2, 2)
+        at(after, 0, 4, x_prod, 2, 3)
         at(after, 0, 4, norm_turn, 1)
         at(before, 0, 5, norm_quant, 1)
         at(after, 0, 7, x_turns, 2)
         at(after, 0, 8, x_quants, 2)
         for b in (1, 2):
             at(after, b, 1, down, b + 1)
+            at(before, b, 2, rbias, b + 1)
             at(before, b, 2, rnorm, b + 1)
             at(before, b, 2, n_make, b + 1, 0)
             at(after, b, 2, n_make, b + 1, 1)

@@ -64,10 +64,10 @@ def tile_mhlattention_pa_w4_kernel(
 
         def load_scales(dst, src, runs, n):
             for g0, g1 in runs:
-                for q in range(4):
+                for r in range(4):
                     nc.sync.dma_start(
-                        out=dst[32 * q:32 * q + 4, n * g0:n * g1].bitcast(I32).rearrange("p (g n) -> p g n", g=g1 - g0),
-                        in_=src[g0:g1, 4 * q:4 * q + 4, :].bitcast(I32).rearrange("g r n -> r g n"),
+                        out=dst[r:P:32, n * g0:n * g1].bitcast(I32).rearrange("q (g n) -> q g n", g=g1 - g0),
+                        in_=src[g0:g1, r:16:4, :].bitcast(I32).rearrange("g q n -> q g n"),
                     )
 
         def load_wd(c):
@@ -84,10 +84,10 @@ def tile_mhlattention_pa_w4_kernel(
         nc.gpsimd.memset(wus[:, 9216:].bitcast(I32), 0)
         nc.vector.memset(wus[:, 0:9216].bitcast(I32), 0)
         make_identity(nc, ident[:])
-        load_scales(wds, w_down_scales, [(0, G1)], LAT)
         load_wd(1)
-        load_wd(2)
         load_x(1)
+        load_scales(wds, w_down_scales, [(0, G1)], LAT)
+        load_wd(2)
         nc.gpsimd.iota(pos[:], pattern=[[P, NB]], base=0, channel_multiplier=1, allow_small_or_imprecise_dtypes=True)
 
         ang = keep.tile([P, NB, PAIRS], F32, name="ang")
@@ -111,7 +111,7 @@ def tile_mhlattention_pa_w4_kernel(
             else:
                 nc.vector.scalar_tensor_tensor(out=red[:], in0=turns[:], scalar=-TWO_PI_LO, in1=red[:], op0=ALU.mult, op1=ALU.add)
 
-        load_scales(wus, w_up_scales, [(0, 1), (1, 2), (2, 3)], D_OUT)
+        load_scales(wus, w_up_scales, [(0, G2)], D_OUT)
 
         def load_wu(j):
             nc.sync.dma_start(out=wu[j][:], in_=w_up_words[:, :, 1024 * j:1024 * (j + 1)].rearrange("g p n -> p g n"))

@@ -25,6 +25,7 @@ G2 = LAT // 512
 ROT = 64
 PAIRS = ROT // 2
 EPS = 1e-6
+WUS_V = 5760
 TWO_PI_HI = 6.28125
 TWO_PI_LO = 2.0 * math.pi - TWO_PI_HI
 
@@ -47,10 +48,8 @@ def tile_mhlattention_pa_w4_kernel(
         pos = keep.tile([P, NB], F32, name="pos")
         warm = keep.tile([P, 1], F32, name="warm")
         vs = keep.tile([P, G1 * 4], F32, name="vs")
-        gain = keep.tile([P, LAT], BF16, name="gain")
-        ones = keep.tile([P, P], BF16, name="ones")
         sx = keep.tile([P, D_MODEL], F32, name="sx")
-        wg = keep.tile([P, LAT], F32, name="wg")
+        wg = keep.tile([P, LAT], BF16, name="wg")
         xb = [keep.tile([P, D_MODEL], U8, name="xb%d" % b) for b in range(NB)]
         wd = [keep.tile([P, G1, 1024], U8, name="wd%d" % c, align_bytes=64) for c in range(G2)]
         wds = keep.tile([P, G1 * LAT], U8, name="wds", align_bytes=64)
@@ -74,20 +73,18 @@ def tile_mhlattention_pa_w4_kernel(
             nc.sync.dma_start(out=wd[c][:], in_=w_down_words[:, :, 1024 * c:1024 * (c + 1)].rearrange("g p n -> p g n"))
 
         load_x(0)
+        load_wd(0)
         nc.vector.memset(warm[:], 0.0)
         nc.scalar.activation(out=warm[:], in_=warm[:], func=ACT.Sin)
-        nc.vector.memset(gain[:], 0.0)
-        nc.vector.memset(ones[:], 1.0)
-        nc.sync.dma_start(out=gain[0:1, :], in_=rms_w.unsqueeze(0))
-        load_wd(0)
         nc.vector.memset(wds[:].bitcast(I32), 0)
-        nc.gpsimd.memset(wus[:, 9216:].bitcast(I32), 0)
-        nc.vector.memset(wus[:, 0:9216].bitcast(I32), 0)
         make_identity(nc, ident[:])
-        load_wd(1)
-        load_x(1)
+        nc.gpsimd.memset(wus[:, WUS_V:].bitcast(I32), 0)
+        nc.vector.memset(wus[:, 0:WUS_V].bitcast(I32), 0)
         load_scales(wds, w_down_scales, [(0, G1)], LAT)
+        load_wd(1)
         load_wd(2)
+        load_x(1)
+        nc.sync.dma_start(out=wg[:], in_=rms_w.partition_broadcast(P))
         nc.gpsimd.iota(pos[:], pattern=[[P, NB]], base=0, channel_multiplier=1, allow_small_or_imprecise_dtypes=True)
 
         ang = keep.tile([P, NB, PAIRS], F32, name="ang")
@@ -97,19 +94,14 @@ def tile_mhlattention_pa_w4_kernel(
             nc.gpsimd.tensor_scalar(out=ang[:, :, n:2 * n], in0=ang[:, :, 0:n], scalar1=10000.0 ** (-n / PAIRS), scalar2=0.0, op0=ALU.mult, op1=ALU.add)
             n = 2 * n
         turns_i = keep.tile([P, NB * PAIRS], I32, name="turns_i")
-        turns = keep.tile([P, NB * PAIRS], F32, name="turns")
         red = keep.tile([P, NB * PAIRS], F32, name="red")
         ang_f = ang[:].rearrange("p b i -> p (b i)")
+        nc.gpsimd.tensor_scalar(out=turns_i[:], in0=ang_f, scalar1=1.0 / (2.0 * math.pi), scalar2=0.0, op0=ALU.mult, op1=ALU.add)
 
         def rope_reduce(step):
-            if step == 0:
-                nc.vector.tensor_scalar(out=turns_i[:], in0=ang_f, scalar1=1.0 / (2.0 * math.pi), scalar2=None, op0=ALU.mult)
-            elif step == 1:
-                nc.vector.tensor_copy(out=turns[:], in_=turns_i[:])
-            elif step == 2:
-                nc.vector.scalar_tensor_tensor(out=red[:], in0=turns[:], scalar=-TWO_PI_HI, in1=ang_f, op0=ALU.mult, op1=ALU.add)
-            else:
-                nc.vector.scalar_tensor_tensor(out=red[:], in0=turns[:], scalar=-TWO_PI_LO, in1=red[:], op0=ALU.mult, op1=ALU.add)
+            nc.vector.scalar_tensor_tensor(
+                out=red[:], in0=turns_i[:], scalar=-TWO_PI_HI if step == 0 else -TWO_PI_LO,
+                in1=ang_f if step == 0 else red[:], op0=ALU.mult, op1=ALU.add)
 
         load_scales(wus, w_up_scales, [(0, G2)], D_OUT)
 
@@ -126,26 +118,25 @@ def tile_mhlattention_pa_w4_kernel(
         s2 = keep.tile([P, NB * PAIRS], F32, name="s2")
         s4 = keep.tile([P, NB * PAIRS], F32, name="s4")
         c2 = keep.tile([P, NB * PAIRS], F32, name="c2")
-        cosd = keep.tile([P, NB, PAIRS, 2], F32, name="cosd")
-        sind = keep.tile([P, NB, PAIRS, 2], F32, name="sind")
+        cosd = keep.tile([P, NB, PAIRS], F32, name="cosd")
+        sind = keep.tile([P, 2, NB, PAIRS], F32, name="sind")
 
         def rope_sines():
             nc.scalar.activation(out=s2[:], in_=red[:], func=ACT.Sin, scale=0.5)
             nc.scalar.activation(out=s4[:], in_=red[:], func=ACT.Sin, scale=0.25)
             nc.scalar.activation(out=warm[:], in_=warm[:], func=ACT.Sqrt)
 
-        def rope_products():
-            nc.vector.tensor_tensor(out=s4[:], in0=s4[:], in1=s4[:], op=ALU.mult)
-            nc.vector.tensor_scalar(out=c2[:], in0=s4[:], scalar1=-2.0, scalar2=1.0, op0=ALU.mult, op1=ALU.add)
-            nc.vector.tensor_tensor(out=c2[:], in0=c2[:], in1=s2[:], op=ALU.mult)
-            nc.vector.tensor_tensor(out=s2[:], in0=s2[:], in1=s2[:], op=ALU.mult)
-
-        def rope_tables():
-            s2_v = s2[:].rearrange("p (b i) -> p b i", b=NB)
-            c2_v = c2[:].rearrange("p (b i) -> p b i", b=NB)
-            for e in range(2):
-                nc.vector.tensor_scalar(out=cosd[:, :, :, e], in0=s2_v, scalar1=-2.0, scalar2=1.0, op0=ALU.mult, op1=ALU.add)
-                nc.vector.tensor_scalar(out=sind[:, :, :, e], in0=c2_v, scalar1=2.0 - 4.0 * e, scalar2=None, op0=ALU.mult)
+        def rope_tables(step):
+            if step == 0:
+                nc.scalar.activation(out=s4[:], in_=s4[:], func=ACT.Square)
+                nc.scalar.activation(out=c2[:], in_=s4[:], func=ACT.Identity, scale=-2.0, bias=1.0)
+                nc.scalar.activation(out=s4[:], in_=s2[:], func=ACT.Square)
+                nc.scalar.activation(out=cosd[:].rearrange("p b i -> p (b i)"), in_=s4[:], func=ACT.Identity, scale=-2.0, bias=1.0)
+            elif step == 1:
+                nc.vector.tensor_tensor(out=c2[:], in0=c2[:], in1=s2[:], op=ALU.mult)
+            else:
+                for e in range(2):
+                    nc.scalar.activation(out=sind[:, e].rearrange("p b i -> p (b i)"), in_=c2[:], func=ACT.Copy, scale=2.0 - 4.0 * e)
 
         xc = [keep.tile([P, G1 * P], U32, name="xc%d" % b, align_bytes=64) for b in range(NB)]
         xcs = [keep.tile([P, G1 * P], U8, name="xcs%d" % b, align_bytes=64) for b in range(NB)]
@@ -164,18 +155,10 @@ def tile_mhlattention_pa_w4_kernel(
         def scale_copy(g, bank):
             nc.scalar.copy(out=sx[:, 512 * g:512 * (g + 1)].rearrange("q (p m) -> q p m", m=4), in_=bank[:].rearrange("q m p -> q p m"))
 
-        def gain_spread(g):
-            bank = work.tile([P, 512], F32, tag="w", name="gain%d" % g)
-            nc.tensor.matmul(bank[:], lhsT=ones[:], rhs=gain[:, 512 * g:512 * (g + 1)], start=True, stop=True)
-            return bank
-
-        def gain_copy(g, bank):
-            nc.scalar.copy(out=wg[:, 512 * g:512 * (g + 1)], in_=bank[:])
-
         def warm_up(n):
             bank = work.tile([P, 512], F32, tag="w", name="warmer")
             for i in range(n):
-                nc.tensor.matmul(bank[:], lhsT=ones[:], rhs=gain[:, 0:512], start=True, stop=True)
+                nc.tensor.matmul(bank[:], lhsT=xs[0, 0][:, 0:P], rhs=xs[0, 0][:], start=True, stop=True)
 
         def x_prod(b, g):
             t = flow.tile([P, 512], BF16, tag="xs", name="xs%d_%d" % (b, g), bufs=5)
@@ -223,18 +206,20 @@ def tile_mhlattention_pa_w4_kernel(
         ntt = {}
         ng_t = {}
 
+        def rbias(b):
+            s = keep.tile([P, 1], F32, name="s%d" % b)
+            m = keep.tile([P, 1], F32, name="m%d" % b)
+            nc.scalar.activation(out=s[:], in_=ss[b][:, 0:1], func=ACT.Identity, bias=ss[b][:, 1:2])
+            nc.scalar.activation(out=m[:], in_=s[:], func=ACT.Identity, scale=1.0 / LAT, bias=EPS)
+            mm[b] = m
+
         def square(b, c):
             if c == 0:
                 ss[b] = keep.tile([P, G2], F32, name="ss%d" % b)
             junk = flow.tile([P, 512], BF16, tag="junk", name="junk%d_%d" % (b, c), bufs=2)
             nc.scalar.activation(out=junk[:], in_=hb[b, c][:], func=ACT.Square, accum_out=ss[b][:, c:c + 1])
-
-        def rbias(b):
-            s = keep.tile([P, 1], F32, name="s%d" % b)
-            m = keep.tile([P, 1], F32, name="m%d" % b)
-            nc.vector.tensor_tensor(out=s[:], in0=ss[b][:, 0:1], in1=ss[b][:, 1:2], op=ALU.add)
-            nc.vector.tensor_scalar(out=m[:], in0=s[:], scalar1=1.0 / LAT, scalar2=EPS, op0=ALU.mult, op1=ALU.add)
-            mm[b] = m
+            if c == 1:
+                rbias(b)
 
         def rnorm(b):
             t = keep.tile([P, 1], F32, name="t%d" % b)
@@ -308,15 +293,16 @@ def tile_mhlattention_pa_w4_kernel(
             else:
                 t = flow.tile([P, HEADS, P], F32, tag="or", name="or%d_%d" % (b, part), bufs=3)
                 turned = flow.tile([P, HEADS, PAIRS, 2], F32, tag="rt", name="rt%d_%d" % (b, part), bufs=2)
-                straight = flow.tile([P, HEADS, ROT], F32, tag="rs", name="rs%d_%d" % (b, part), bufs=2)
-                cos_b = cosd[:, b].rearrange("p i e -> p (i e)").unsqueeze(1).to_broadcast([P, HEADS, ROT])
-                sin_b = sind[:, b].rearrange("p i e -> p (i e)").unsqueeze(1).to_broadcast([P, HEADS, ROT])
-                nc.vector.tensor_tensor(out=straight[:], in0=heads[:, :, 0:ROT], in1=cos_b, op=ALU.mult)
-                nc.vector.tensor_tensor(out=turned[:].rearrange("p h i e -> p h (i e)"), in0=heads[:, :, 0:ROT], in1=sin_b, op=ALU.mult)
+                straight = flow.tile([P, HEADS, PAIRS, 2], F32, tag="rs", name="rs%d_%d" % (b, part), bufs=2)
+                pairs = heads[:, :, 0:ROT].rearrange("p h (i e) -> p h i e", e=2)
+                cos_b = cosd[:, b].unsqueeze(1).unsqueeze(3).to_broadcast([P, HEADS, PAIRS, 2])
+                sin_b = sind[:, :, b].rearrange("p e i -> p i e").unsqueeze(1).to_broadcast([P, HEADS, PAIRS, 2])
+                nc.vector.tensor_tensor(out=straight[:], in0=pairs, in1=cos_b, op=ALU.mult)
+                nc.vector.tensor_tensor(out=turned[:], in0=pairs, in1=sin_b, op=ALU.mult)
                 nc.scalar.copy(out=t[:, :, ROT:P], in_=heads[:, :, ROT:P])
                 nc.vector.tensor_tensor(
                     out=t[:, :, 0:ROT].rearrange("p h (i e) -> p h i e", e=2),
-                    in0=straight[:].rearrange("p h (i e) -> p h i e", e=2), in1=turned[:, :, :, ::-1], op=ALU.add)
+                    in0=straight[:], in1=turned[:, :, :, ::-1], op=ALU.add)
                 dst = q_rope if part == 0 else k_rope
                 nc.sync.dma_start(out=dst[0, :, rows, :].rearrange("h p d -> p h d"), in_=t[:])
 
@@ -332,68 +318,68 @@ def tile_mhlattention_pa_w4_kernel(
         last = scale_spread(3)
         scale_copy(3, last)
         x_prod(0, 1)
-        rope_reduce(0)
         x_quant(0, 0, 1)
         x_turn(0, 1, 1)
         x_copy(0, 1, 1, act)
         warm_up(1)
         x_prod(0, 2)
-        rope_reduce(1)
+        rope_reduce(0)
         x_quant(0, 1, 1)
         x_turn(0, 2, 1)
         x_copy(0, 2, 1, act)
-        warm_up(1)
         x_prod(0, 3)
-        rope_reduce(2)
         x_quant(0, 2, 1)
+        h_open(0)
+        for c in range(2):
+            for g in range(2):
+                h_mm(0, c, g)
         x_turn(0, 3, 1)
-        rope_reduce(3)
+        rope_reduce(1)
         x_copy(0, 3, 1, act)
         x_quant(0, 3, 1)
         x_prod(1, 0)
         rope_sines()
-        gains = [gain_spread(g) for g in range(G2)]
-        h_open(0)
         for c in range(2):
-            for g in range(G1):
+            for g in range(2, G1):
                 h_mm(0, c, g)
             square(0, c)
         x_prod(1, 1)
         x_turn(1, 0, 2)
+        x_copy(1, 0, 2, act)
         x_prod(1, 2)
-        x_copy(1, 0, 2, vec)
-        gain_copy(0, gains[0])
-        for g in range(G1):
-            h_mm(0, 2, g)
         x_prod(1, 3)
         x_quant(1, 0, 2)
-        rbias(0)
+        for g in range(G1):
+            h_mm(0, 2, g)
         x_turn(1, 2, 2)
-        x_copy(1, 2, 2, vec)
         square(0, 2)
+        x_copy(1, 2, 2, act)
         x_quant(1, 2, 2)
         rnorm(0)
-        gain_copy(1, gains[1])
-        gain_copy(2, gains[2])
+        rope_tables(0)
         n_make(0, 0)
         n_make(0, 1)
         n_make(0, 2)
         h_open(1)
         for c in range(2):
-            for g in range(G1):
+            for g in range(2):
                 h_mm(1, c, g)
+        for c in range(2):
+            for g in range(2, G1):
+                h_mm(1, c, g)
+            square(1, c)
         n_turn(0, 0, 2)
         n_turn(0, 2, 1)
-        n_copy(0, 0, 2, act)
-        n_copy(0, 2, 1, vec)
-        square(1, 0)
+        n_copy(0, 0, 2, vec)
+        n_copy(0, 2, 1, act)
         n_quant(0, 0, 2)
         n_quant(0, 2, 1)
         for g in range(G1):
             h_mm(1, 2, g)
-        square(1, 1)
         square(1, 2)
-        rope_products()
+        rope_tables(1)
+        rnorm(1)
+        rope_tables(2)
 
         def norm_turn(b):
             n_turn(b, 0, 2)
@@ -428,13 +414,10 @@ def tile_mhlattention_pa_w4_kernel(
         def at(table, b, j, fn, *args):
             table.setdefault((b, j), []).append((fn, args))
 
-        at(before, 0, 0, x_prod, 2, 0)
-        at(before, 0, 0, rbias, 1)
-        at(before, 0, 0, rnorm, 1)
-        at(after, 0, 0, n_make, 1, 0)
+        at(before, 0, 0, n_make, 1, 0)
         at(after, 0, 0, n_make, 1, 1)
-        at(after, 0, 1, n_make, 1, 2)
-        at(after, 0, 1, rope_tables)
+        at(after, 0, 0, n_make, 1, 2)
+        at(after, 0, 1, x_prod, 2, 0)
         at(after, 0, 2, x_prod, 2, 1)
         at(after, 0, 3, x_prod, 2, 2)
         at(after, 0, 4, x_prod, 2, 3)
@@ -444,10 +427,9 @@ def tile_mhlattention_pa_w4_kernel(
         at(after, 0, 8, x_quants, 2)
         for b in (1, 2):
             at(after, b, 1, down, b + 1)
-            at(before, b, 2, rbias, b + 1)
             at(before, b, 2, rnorm, b + 1)
             at(before, b, 2, n_make, b + 1, 0)
-            at(after, b, 2, n_make, b + 1, 1)
+            at(before, b, 2, n_make, b + 1, 1)
             at(after, b, 3, n_make, b + 1, 2)
             at(after, b, 6, norm_turn, b + 1)
             at(after, b, 7, norm_quant, b + 1)

import math
from contextlib import ExitStack

import concourse.mybir as mybir
from concourse.masks import make_identity

F32 = mybir.dt.float32
BF16 = mybir.dt.bfloat16
I32 = mybir.dt.int32
U32 = mybir.dt.uint32
U8 = mybir.dt.uint8
FP8 = mybir.dt.float8_e4m3fn
FP8X4 = mybir.dt.float8_e4m3fn_x4
FP4X4 = mybir.dt.float4_e2m1fn_x4
ALU = mybir.AluOpType
ACT = mybir.ActivationFunctionType
AX = mybir.AxisListType

P = 128
S, D_MODEL, LAT, HEADS, D_HEAD = 512, 2048, 1536, 4, 384
D_OUT = 3 * HEADS * D_HEAD
NB = S // P
G1 = D_MODEL // 512
G2 = LAT // 512
ROT = 64
PAIRS = ROT // 2
EPS = 1e-6
WUS_V = 5760
TWO_PI_HI = 6.28125
TWO_PI_LO = 2.0 * math.pi - TWO_PI_HI

FLOPS = 2 * S * D_MODEL * LAT + 2 * S * LAT * D_OUT


def tile_mhlattention_pa_w4_kernel(
    tc, x_bytes, x_scale, w_down_words, w_down_scales, rms_w, w_up_words, w_up_scales,
    q_nope, q_rope, k_nope, k_rope, v_out,
):
    nc = tc.nc
    with ExitStack() as ctx:
        keep = ctx.enter_context(tc.tile_pool(name="keep", bufs=1))
        flow = ctx.enter_context(tc.tile_pool(name="flow", bufs=3))
        work = ctx.enter_context(tc.psum_pool(name="work", bufs=6))
        turn = ctx.enter_context(tc.psum_pool(name="turn", bufs=2))
        ctx.enter_context(tc.manual_schedule())

        ident = keep.tile([P, P], F32, name="ident")
        pos = keep.tile([P, NB], F32, name="pos")
        warm = keep.tile([P, 1], F32, name="warm")
        vs = keep.tile([P, G1 * 4], F32, name="vs")
        sx = keep.tile([P, D_MODEL], F32, name="sx")
        wg = keep.tile([P, LAT], BF16, name="wg")
        xb = [keep.tile([P, D_MODEL], U8, name="xb%d" % b) for b in range(NB)]
        wd = [keep.tile([P, G1, 1024], U8, name="wd%d" % c, align_bytes=64) for c in range(G2)]
        wds = keep.tile([P, G1 * LAT], U8, name="wds", align_bytes=64)
        wu = [keep.tile([P, G2, 1024], U8, name="wu%d" % j, align_bytes=64) for j in range(9)]
        wus = keep.tile([P, G2 * D_OUT], U8, name="wus", align_bytes=64)

        nc.sync.dma_start(out=vs[:].rearrange("p (g m) -> p g m", m=4), in_=x_scale.rearrange("a o (g p m) -> p (a o g) m", p=P, m=4))

        def load_x(b):
            nc.sync.dma_start(out=xb[b][:], in_=x_bytes[0, b * P:(b + 1) * P, :])

        def load_scales(dst, src, runs, n):
            for g0, g1 in runs:
                for r in range(4):
                    nc.sync.dma_start(
                        out=dst[r:P:32, n * g0:n * g1].bitcast(I32).rearrange("q (g n) -> q g n", g=g1 - g0),
                        in_=src[g0:g1, r:16:4, :].bitcast(I32).rearrange("g q n -> q g n"),
                    )

        def load_wd(c):
            nc.sync.dma_start(out=wd[c][:], in_=w_down_words[:, :, 1024 * c:1024 * (c + 1)].rearrange("g p n -> p g n"))

        load_x(0)
        load_wd(0)
        nc.vector.memset(warm[:], 0.0)
        nc.scalar.activation(out=warm[:], in_=warm[:], func=ACT.Sin)
        nc.vector.memset(wds[:].bitcast(I32), 0)
        make_identity(nc, ident[:])
        nc.gpsimd.memset(wus[:, WUS_V:].bitcast(I32), 0)
        nc.vector.memset(wus[:, 0:WUS_V].bitcast(I32), 0)
        load_scales(wds, w_down_scales, [(0, G1)], LAT)
        load_wd(1)
        load_wd(2)
        load_x(1)
        nc.sync.dma_start(out=wg[:], in_=rms_w.partition_broadcast(P))
        nc.gpsimd.iota(pos[:], pattern=[[P, NB]], base=0, channel_multiplier=1, allow_small_or_imprecise_dtypes=True)

        ang = keep.tile([P, NB, PAIRS], F32, name="ang")
        nc.gpsimd.tensor_scalar(out=ang[:, :, 0:1], in0=pos[:].unsqueeze(2), scalar1=1.0, scalar2=0.0, op0=ALU.mult, op1=ALU.add)
        n = 1
        while n < PAIRS:
            nc.gpsimd.tensor_scalar(out=ang[:, :, n:2 * n], in0=ang[:, :, 0:n], scalar1=10000.0 ** (-n / PAIRS), scalar2=0.0, op0=ALU.mult, op1=ALU.add)
            n = 2 * n
        turns_i = keep.tile([P, NB * PAIRS], I32, name="turns_i")
        red = keep.tile([P, NB * PAIRS], F32, name="red")
        ang_f = ang[:].rearrange("p b i -> p (b i)")
        nc.gpsimd.tensor_scalar(out=turns_i[:], in0=ang_f, scalar1=1.0 / (2.0 * math.pi), scalar2=0.0, op0=ALU.mult, op1=ALU.add)

        def rope_reduce(step):
            nc.vector.scalar_tensor_tensor(
                out=red[:], in0=turns_i[:], scalar=-TWO_PI_HI if step == 0 else -TWO_PI_LO,
                in1=ang_f if step == 0 else red[:], op0=ALU.mult, op1=ALU.add)

        load_scales(wus, w_up_scales, [(0, G2)], D_OUT)

        def load_wu(j):
            nc.sync.dma_start(out=wu[j][:], in_=w_up_words[:, :, 1024 * j:1024 * (j + 1)].rearrange("g p n -> p g n"))

        load_wu(0)
        load_wu(1)
        load_x(2)
        for j in range(2, 9):
            load_wu(j)
        load_x(3)

        s2 = keep.tile([P, NB * PAIRS], F32, name="s2")
        s4 = keep.tile([P, NB * PAIRS], F32, name="s4")
        c2 = keep.tile([P, NB * PAIRS], F32, name="c2")
        cosd = keep.tile([P, NB, PAIRS], F32, name="cosd")
        sind = keep.tile([P, 2, NB, PAIRS], F32, name="sind")

        def rope_sines():
            nc.scalar.activation(out=s2[:], in_=red[:], func=ACT.Sin, scale=0.5)
            nc.scalar.activation(out=s4[:], in_=red[:], func=ACT.Sin, scale=0.25)
            nc.scalar.activation(out=warm[:], in_=warm[:], func=ACT.Sqrt)

        def rope_tables(step):
            if step == 0:
                nc.scalar.activation(out=s4[:], in_=s4[:], func=ACT.Square)
                nc.scalar.activation(out=c2[:], in_=s4[:], func=ACT.Identity, scale=-2.0, bias=1.0)
                nc.scalar.activation(out=s4[:], in_=s2[:], func=ACT.Square)
                nc.scalar.activation(out=cosd[:].rearrange("p b i -> p (b i)"), in_=s4[:], func=ACT.Identity, scale=-2.0, bias=1.0)
            elif step == 1:
                nc.vector.tensor_tensor(out=c2[:], in0=c2[:], in1=s2[:], op=ALU.mult)
            else:
                for e in range(2):
                    nc.scalar.activation(out=sind[:, e].rearrange("p b i -> p (b i)"), in_=c2[:], func=ACT.Copy, scale=2.0 - 4.0 * e)

        xc = [keep.tile([P, G1 * P], U32, name="xc%d" % b, align_bytes=64) for b in range(NB)]
        xcs = [keep.tile([P, G1 * P], U8, name="xcs%d" % b, align_bytes=64) for b in range(NB)]
        nq = [keep.tile([P, G2 * P], U32, name="nq%d" % b, align_bytes=64) for b in range(NB)]
        nqs = [keep.tile([P, G2 * P], U8, name="nqs%d" % b, align_bytes=64) for b in range(NB)]
        xs = {}
        xt = {}
        xg = {}

        def scale_spread(g):
            bank = work.tile([P, 4, P], F32, tag="w", name="spread%d" % g)
            for m in range(4):
                nc.tensor.transpose(bank[:, m, :], vs[:, 4 * g + m:4 * g + m + 1].to_broadcast([P, P]), ident[:])
            return bank

        def scale_copy(g, bank):
            nc.scalar.copy(out=sx[:, 512 * g:512 * (g + 1)].rearrange("q (p m) -> q p m", m=4), in_=bank[:].rearrange("q m p -> q p m"))

        def warm_up(n):
            bank = work.tile([P, 512], F32, tag="w", name="warmer")
            for i in range(n):
                nc.tensor.matmul(bank[:], lhsT=xs[0, 0][:, 0:P], rhs=xs[0, 0][:], start=True, stop=True)

        def x_prod(b, g):
            t = flow.tile([P, 512], BF16, tag="xs", name="xs%d_%d" % (b, g), bufs=5)
            nc.vector.tensor_tensor(out=t[:], in0=xb[b][:, 512 * g:512 * (g + 1)].bitcast(FP8), in1=sx[:, 512 * g:512 * (g + 1)], op=ALU.mult)
            xs[b, g] = t

        def x_turn(b, g0, ng):
            t = turn.tile([P, 2, 2, P], F32, tag="t", name="xt%d_%d" % (b, g0))
            for g in range(ng):
                words = xs[b, g0 + g][:].bitcast(F32)
                for u in range(2):
                    nc.tensor.transpose(t[:, g, u, :], words[:, u:256:2], ident[:])
            xt[b, g0] = t

        def x_copy(b, g0, ng, copy):
            t = flow.tile([P, 2, P, 4], BF16, tag="xg", name="xg%d_%d" % (b, g0), bufs=4, align_bytes=64)
            dst = t[:, 0:ng].rearrange("p g n t -> p (g n t)").bitcast(F32).rearrange("p (g n u) -> p g n u", g=ng, u=2)
            copy(out=dst, in_=xt[b, g0][:, 0:ng].rearrange("p g u n -> p g n u"))
            xg[b, g0] = t

        def x_quant(b, g0, ng):
            cols = slice(P * g0, P * (g0 + ng))
            nc.vector.quantize_mx(out=xc[b][:, cols].bitcast(FP8X4), scales=xcs[b][:, cols], in_=xg[b, g0][:, 0:ng].rearrange("p g n t -> p (g n t)"))

        hb = {}

        def h_open(b):
            for c in range(G2):
                t = work.tile([P, 512], F32, tag="w", name="h%d_%d" % (b, c))
                hb[b, c] = t

        def h_mm(b, c, g):
            cols = slice(P * g, P * (g + 1))
            nc.tensor.matmul_mx(
                out=hb[b, c][:],
                lhsT=xc[b][:, cols].bitcast(FP8X4), lhsT_scale=xcs[b][:, cols],
                rhs=wd[c][:, g, :].bitcast(FP4X4), rhs_scale=wds[:, LAT * g + 512 * c:LAT * g + 512 * (c + 1)],
                start=(g == 0), stop=(g == G1 - 1),
            )

        ss = {}
        rr = {}
        mm = {}
        nt = {}
        ntt = {}
        ng_t = {}

        def rbias(b):
            s = keep.tile([P, 1], F32, name="s%d" % b)
            m = keep.tile([P, 1], F32, name="m%d" % b)
            nc.scalar.activation(out=s[:], in_=ss[b][:, 0:1], func=ACT.Identity, bias=ss[b][:, 1:2])
            nc.scalar.activation(out=m[:], in_=s[:], func=ACT.Identity, scale=1.0 / LAT, bias=EPS)
            mm[b] = m

        def square(b, c):
            if c == 0:
                ss[b] = keep.tile([P, G2], F32, name="ss%d" % b)
            junk = flow.tile([P, 512], BF16, tag="junk", name="junk%d_%d" % (b, c), bufs=2)
            nc.scalar.activation(out=junk[:], in_=hb[b, c][:], func=ACT.Square, accum_out=ss[b][:, c:c + 1])
            if c == 1:
                rbias(b)

        def rnorm(b):
            t = keep.tile([P, 1], F32, name="t%d" % b)
            r = keep.tile([P, 1], F32, name="r%d" % b)
            nc.scalar.activation(out=t[:], in_=ss[b][:, 2:3], func=ACT.Sqrt, scale=1.0 / LAT, bias=mm[b][:])
            nc.vector.reciprocal(out=r[:], in_=t[:])
            rr[b] = r

        def n_make(b, g):
            t = flow.tile([P, 2, P, 2], BF16, tag="n", name="n%d_%d" % (b, g), bufs=5)
            hv = hb[b, g][:].rearrange("p (c u e) -> p u c e", u=2, e=2)
            wv = wg[:, 512 * g:512 * (g + 1)].rearrange("p (c u e) -> p u c e", u=2, e=2)
            for u in range(2):
                nc.vector.scalar_tensor_tensor(out=t[:, u], in0=hv[:, u], scalar=rr[b][:], in1=wv[:, u], op0=ALU.mult, op1=ALU.mult)
            nt[b, g] = t

        def n_turn(b, g0, ng):
            t = turn.tile([P, 2, 2, P], F32, tag="t", name="nt%d_%d" % (b, g0))
            for g in range(ng):
                words = nt[b, g0 + g][:].rearrange("p u c e -> p (u c e)").bitcast(F32)
                for u in range(2):
                    nc.tensor.transpose(t[:, g, u, :], words[:, P * u:P * (u + 1)], ident[:])
            ntt[b, g0] = t

        def n_copy(b, g0, ng, copy):
            t = flow.tile([P, 2, P, 4], BF16, tag="xg", name="ng%d_%d" % (b, g0), bufs=4, align_bytes=64)
            dst = t[:, 0:ng].rearrange("p g n t -> p (g n t)").bitcast(F32).rearrange("p (g n u) -> p g n u", g=ng, u=2)
            copy(out=dst, in_=ntt[b, g0][:, 0:ng].rearrange("p g u n -> p g n u"))
            ng_t[b, g0] = t

        def n_quant(b, g0, ng):
            cols = slice(P * g0, P * (g0 + ng))
            nc.vector.quantize_mx(out=nq[b][:, cols].bitcast(FP8X4), scales=nqs[b][:, cols], in_=ng_t[b, g0][:, 0:ng].rearrange("p g n t -> p (g n t)"))

        ob = {}
        ot = {}

        def up_mm(b, j):
            t = work.tile([P, 512], F32, tag="w", name="o%d_%d" % (b, j))
            for g in range(G2):
                cols = slice(P * g, P * (g + 1))
                nc.tensor.matmul_mx(
                    out=t[:],
                    lhsT=nq[b][:, cols].bitcast(FP8X4), lhsT_scale=nqs[b][:, cols],
                    rhs=wu[j][:, g, :].bitcast(FP4X4), rhs_scale=wus[:, D_OUT * g + 512 * j:D_OUT * g + 512 * (j + 1)],
                    start=(g == 0), stop=(g == G2 - 1),
                )
            ob[b, j] = t

        def evacuate(b, j, copy):
            rows = slice(P * b, P * (b + 1))
            heads = ob[b, j][:].rearrange("p (d h) -> p h d", h=HEADS)
            part, c = divmod(j, 3)
            if part == 2:
                if c == 0:
                    ot[b, "v"] = flow.tile([P, HEADS, 384], F32, tag="ov", name="ov%d" % b, bufs=2)
                t = ot[b, "v"]
                copy(out=t[:, :, P * c:P * (c + 1)], in_=heads)
                if b == NB - 1:
                    nc.sync.dma_start(out=v_out[0, :, rows, P * c:P * (c + 1)].rearrange("h p d -> p h d"), in_=t[:, :, P * c:P * (c + 1)])
                elif c == 2:
                    nc.sync.dma_start(out=v_out[0, :, rows, :].rearrange("h p d -> p h d"), in_=t[:])
            elif c < 2:
                if c == 0:
                    ot[b, part] = flow.tile([P, HEADS, 256], F32, tag="on", name="on%d_%d" % (b, part), bufs=3)
                t = ot[b, part]
                copy(out=t[:, :, P * c:P * (c + 1)], in_=heads)
                if c == 1:
                    dst = q_nope if part == 0 else k_nope
                    nc.sync.dma_start(out=dst[0, :, rows, :].rearrange("h p d -> p h d"), in_=t[:])
            else:
                t = flow.tile([P, HEADS, P], F32, tag="or", name="or%d_%d" % (b, part), bufs=3)
                turned = flow.tile([P, HEADS, PAIRS, 2], F32, tag="rt", name="rt%d_%d" % (b, part), bufs=2)
                straight = flow.tile([P, HEADS, PAIRS, 2], F32, tag="rs", name="rs%d_%d" % (b, part), bufs=2)
                pairs = heads[:, :, 0:ROT].rearrange("p h (i e) -> p h i e", e=2)
                cos_b = cosd[:, b].unsqueeze(1).unsqueeze(3).to_broadcast([P, HEADS, PAIRS, 2])
                sin_b = sind[:, :, b].rearrange("p e i -> p i e").unsqueeze(1).to_broadcast([P, HEADS, PAIRS, 2])
                nc.vector.tensor_tensor(out=straight[:], in0=pairs, in1=cos_b, op=ALU.mult)
                nc.vector.tensor_tensor(out=turned[:], in0=pairs, in1=sin_b, op=ALU.mult)
                nc.scalar.copy(out=t[:, :, ROT:P], in_=heads[:, :, ROT:P])
                nc.vector.tensor_tensor(
                    out=t[:, :, 0:ROT].rearrange("p h (i e) -> p h i e", e=2),
                    in0=straight[:], in1=turned[:, :, :, ::-1], op=ALU.add)
                dst = q_rope if part == 0 else k_rope
                nc.sync.dma_start(out=dst[0, :, rows, :].rearrange("h p d -> p h d"), in_=t[:])

        act = nc.scalar.copy
        vec = nc.vector.tensor_copy

        spread = [scale_spread(g) for g in range(3)]
        for g in range(3):
            scale_copy(g, spread[g])
        x_prod(0, 0)
        x_turn(0, 0, 1)
        x_copy(0, 0, 1, act)
        last = scale_spread(3)
        scale_copy(3, last)
        x_prod(0, 1)
        x_quant(0, 0, 1)
        x_turn(0, 1, 1)
        x_copy(0, 1, 1, act)
        warm_up(1)
        x_prod(0, 2)
        rope_reduce(0)
        x_quant(0, 1, 1)
        x_turn(0, 2, 1)
        x_copy(0, 2, 1, act)
        x_prod(0, 3)
        x_quant(0, 2, 1)
        h_open(0)
        for c in range(2):
            for g in range(2):
                h_mm(0, c, g)
        x_turn(0, 3, 1)
        rope_reduce(1)
        x_copy(0, 3, 1, act)
        x_quant(0, 3, 1)
        x_prod(1, 0)
        rope_sines()
        for c in range(2):
            for g in range(2, G1):
                h_mm(0, c, g)
            square(0, c)
        x_prod(1, 1)
        x_turn(1, 0, 2)
        x_copy(1, 0, 2, act)
        x_prod(1, 2)
        x_prod(1, 3)
        x_quant(1, 0, 2)
        for g in range(G1):
            h_mm(0, 2, g)
        x_turn(1, 2, 2)
        square(0, 2)
        x_copy(1, 2, 2, act)
        x_quant(1, 2, 2)
        rnorm(0)
        rope_tables(0)
        n_make(0, 0)
        n_make(0, 1)
        n_make(0, 2)
        h_open(1)
        for c in range(2):
            for g in range(2):
                h_mm(1, c, g)
        for c in range(2):
            for g in range(2, G1):
                h_mm(1, c, g)
            square(1, c)
        n_turn(0, 0, 2)
        n_turn(0, 2, 1)
        n_copy(0, 0, 2, vec)
        n_copy(0, 2, 1, act)
        n_quant(0, 0, 2)
        n_quant(0, 2, 1)
        for g in range(G1):
            h_mm(1, 2, g)
        square(1, 2)
        rope_tables(1)
        rnorm(1)
        rope_tables(2)

        def norm_turn(b):
            n_turn(b, 0, 2)
            n_turn(b, 2, 1)
            n_copy(b, 0, 2, act)
            n_copy(b, 2, 1, act)

        def norm_quant(b):
            n_quant(b, 0, 2)
            n_quant(b, 2, 1)

        def x_turns(b):
            x_turn(b, 0, 2)
            x_turn(b, 2, 2)
            x_copy(b, 0, 2, act)
            x_copy(b, 2, 2, act)

        def x_quants(b):
            x_quant(b, 0, 2)
            x_quant(b, 2, 2)

        def down(b):
            h_open(b)
            for c in range(G2):
                for g in range(G1):
                    h_mm(b, c, g)
                square(b, c)

        before = {}
        after = {}

        def at(table, b, j, fn, *args):
            table.setdefault((b, j), []).append((fn, args))

        at(before, 0, 0, n_make, 1, 0)
        at(after, 0, 0, n_make, 1, 1)
        at(after, 0, 0, n_make, 1, 2)
        at(after, 0, 1, x_prod, 2, 0)
        at(after, 0, 2, x_prod, 2, 1)
        at(after, 0, 3, x_prod, 2, 2)
        at(after, 0, 4, x_prod, 2, 3)
        at(after, 0, 4, norm_turn, 1)
        at(before, 0, 5, norm_quant, 1)
        at(after, 0, 7, x_turns, 2)
        at(after, 0, 8, x_quants, 2)
        for b in (1, 2):
            at(after, b, 1, down, b + 1)
            at(before, b, 2, rnorm, b + 1)
            at(before, b, 2, n_make, b + 1, 0)
            at(before, b, 2, n_make, b + 1, 1)
            at(after, b, 3, n_make, b + 1, 2)
            at(after, b, 6, norm_turn, b + 1)
            at(after, b, 7, norm_quant, b + 1)
        for g, j in enumerate((0, 0, 1, 1)):
            at(after, 1, j, x_prod, 3, g)
        at(after, 1, 4, x_turns, 3)
        at(after, 1, 5, x_quants, 3)

        for b in range(NB):
            for j in range(9):
                up_mm(b, j)
                for fn, args in before.get((b, j), []):
                    fn(*args)
                evacuate(b, j, vec if b == NB - 1 and j in (1, 4, 7) else act)
                for fn, args in after.get((b, j), []):
                    fn(*args)
